import numpy as np
import ml_dtypes


def mxq(x, axis, fmt="e4m3"):
    dtype, down = {"e4m3": (ml_dtypes.float8_e4m3fn, 7), "e5m2": (ml_dtypes.float8_e5m2, 14)}[fmt]
    v = np.moveaxis(np.asarray(x, np.float32).astype(ml_dtypes.bfloat16).astype(np.float64), axis, -1)
    blocks = v.reshape(v.shape[:-1] + (-1, 32))
    amax = np.abs(blocks).max(-1, keepdims=True)
    byte = np.maximum(np.where(amax > 0, np.frexp(amax)[1] - 1 + 127, 0) - down, 1)
    scale = np.exp2(byte - 127.0)
    codes = (blocks / scale).astype(np.float32).astype(dtype).astype(np.float64)
    return np.moveaxis((codes * scale).reshape(v.shape), -1, axis)


WIDE = False


def mx_kscale(k):
    if not WIDE:
        return np.ones(k)
    levels = np.array([10, -10, 5, -5, 0])
    a = np.random.permutation(np.resize(levels, k // 512 * 4)).reshape(k // 512, 4)
    idx = np.arange(k)
    return np.exp2(a[idx // 512, idx % 128 // 32])


BF16 = ml_dtypes.bfloat16


def bf(x):
    return np.asarray(x, np.float32).astype(BF16)


def f64(x):
    return np.asarray(x).astype(np.float64)


E2M1 = np.array([0.0, 0.5, 1.0, 1.5, 2.0, 3.0, 4.0, 6.0, -0.0, -0.5, -1.0, -1.5, -2.0, -3.0, -4.0, -6.0])


def pack_weight(w, fmt):
    k, n = w.shape
    w = f64(bf(w)).reshape(k // 32, 32, n)
    amax = np.abs(w).max(1)
    if fmt == "e4m3":
        byte = np.frexp(amax)[1] - 1 + 127 - 7
    else:
        mant, ex = np.frexp(amax / 6.0)
        byte = np.where(mant > 0.5, ex, ex - 1) + 127
    byte = np.clip(np.where(amax > 0, byte, 1), 1, 254)
    scaled = (w * np.exp2(127.0 - byte)[:, None, :]).reshape(k, n).astype(np.float32)
    by_word = np.ascontiguousarray(scaled.reshape(k // 512, 128, 4, n).transpose(0, 1, 3, 2))
    if fmt == "e4m3":
        words = by_word.astype(ml_dtypes.float8_e4m3fn).view(np.uint8)
    else:
        c = by_word.astype(ml_dtypes.float4_e2m1fn).view(np.uint8) & 0xF
        words = c[..., 0::2] | (c[..., 1::2] << 4)
    return np.ascontiguousarray(words), np.ascontiguousarray(byte.astype(np.uint8).reshape(k // 512, 16, n))


def unpack_weight(words, scales, fmt):
    g, p, n, _ = words.shape
    if fmt == "e4m3":
        vals = np.ascontiguousarray(words).view(ml_dtypes.float8_e4m3fn).astype(np.float64)
    else:
        nib = np.empty((g, p, n, 4), np.uint8)
        nib[..., 0::2] = words & 0xF
        nib[..., 1::2] = words >> 4
        vals = E2M1[nib]
    vals = vals * np.repeat(np.exp2(scales.astype(np.float64) - 127.0), 8, axis=1)[..., None]
    return vals.transpose(0, 1, 3, 2).reshape(g * 512, n)


B, S, HID, H, G, D, QB = 1, 1024, 1024, 16, 4, 128, 512
ROPE_THETA = 1.0e6
FMT = "e4m3"


def rotate_half(t):
    t1 = t[..., t.shape[-1] // 2:]
    t2 = t[..., : t.shape[-1] // 2]
    return np.concatenate((-t1, t2), axis=-1)


def rope_tables():
    inv_freq = 1.0 / (ROPE_THETA ** (np.arange(0, D, 2) / D))
    freqs = np.arange(S)[:, None] * inv_freq[None, :]
    emb = np.concatenate((freqs, freqs), axis=-1)
    return np.cos(emb), np.sin(emb)


def setup_inputs():
    s = mx_kscale(HID)
    cos, sin = rope_tables()
    x = bf(np.random.standard_normal((B, S, HID)) * s)
    Wq_words, Wq_scales = pack_weight(np.random.standard_normal((HID, H * D)) * 1.5 / np.sqrt(HID) / s[:, None], FMT)
    Wk_words, Wk_scales = pack_weight(np.random.standard_normal((HID, G * D)) * 1.5 / np.sqrt(HID) / s[:, None], FMT)
    Wv_words, Wv_scales = pack_weight(np.random.standard_normal((HID, G * D)) * 1.0 / np.sqrt(HID) / s[:, None], FMT)
    return {"x": x,
            "cos": bf(cos),
            "sin": bf(sin),
            "Wq_words": Wq_words,
            "Wq_scales": Wq_scales,
            "Wk_words": Wk_words,
            "Wk_scales": Wk_scales,
            "Wv_words": Wv_words,
            "Wv_scales": Wv_scales}


def reference(x, cos, sin, Wq_words, Wq_scales, Wk_words, Wk_scales, Wv_words, Wv_scales):
    xq = mxq(f64(x), 2, "e4m3")
    q = (xq @ unpack_weight(Wq_words, Wq_scales, FMT)).reshape(B, S, H, D)
    k = (xq @ unpack_weight(Wk_words, Wk_scales, FMT)).reshape(B, S, G, D)
    v = (xq @ unpack_weight(Wv_words, Wv_scales, FMT)).reshape(B, S, G, D)
    c = f64(cos)[None, :, None, :]
    sn = f64(sin)[None, :, None, :]
    q = q * c + rotate_half(q) * sn
    k = k * c + rotate_half(k) * sn
    return q, k, v

@@ -1,0 +1,193 @@
+from contextlib import ExitStack
+
+import concourse.mybir as mybir
+from concourse.masks import make_identity
+
+F32 = mybir.dt.float32
+BF16 = mybir.dt.bfloat16
+I32 = mybir.dt.int32
+U32 = mybir.dt.uint32
+U8 = mybir.dt.uint8
+FP8X4 = mybir.dt.float8_e4m3fn_x4
+MULT = mybir.AluOpType.mult
+ADD = mybir.AluOpType.add
+
+P = 128
+TOKENS = 1024
+HIDDEN = 1024
+TILES = TOKENS // P
+K_PASS = 4 * P
+PASSES = HIDDEN // K_PASS
+WORDS = K_PASS // 2
+HEAD = 128
+HALF = HEAD // 2
+BANK = 512
+BANK_HEADS = BANK // HEAD
+PAIR = 2
+Q_COLS = 2048
+K_COLS = 512
+V_COLS = 512
+K_START = Q_COLS
+V_START = Q_COLS + K_COLS
+W_COLS = Q_COLS + K_COLS + V_COLS
+
+FLOPS = 2 * TOKENS * HIDDEN * W_COLS
+
+
+def tile_attention_pa_kernel(
+    tc, x, cos, sin, Wq_words, Wq_scales, Wk_words, Wk_scales, Wv_words, Wv_scales, out_0, out_1, out_2
+):
+    nc = tc.nc
+
+    x_rows = x.rearrange("o (r t) k -> r (o t) k", t=TILES)
+    cos_rows = cos.rearrange("(r t) d -> r t d", t=TILES)
+    sin_rows = sin.rearrange("(r t) d -> r t d", t=TILES)
+    q_rows = out_0.rearrange("o (r t) h d -> r (o t) (h d)", t=TILES)
+    k_rows = out_1.rearrange("o (r t) h d -> r (o t) (h d)", t=TILES)
+    v_rows = out_2.rearrange("o (r t) h d -> r (o t) (h d)", t=TILES)
+
+    with ExitStack() as ctx:
+        keep = ctx.enter_context(tc.tile_pool(name="keep", bufs=1))
+        stage = ctx.enter_context(tc.tile_pool(name="stage", bufs=3))
+        turned = ctx.enter_context(tc.psum_pool(name="turned", bufs=2))
+        sums = ctx.enter_context(tc.psum_pool(name="sums", bufs=4))
+        v_sums = ctx.enter_context(tc.psum_pool(name="v_sums", bufs=2))
+        ctx.enter_context(tc.manual_schedule())
+
+        x_sb = keep.tile([P, TILES, HIDDEN], BF16)
+        cos_sb = keep.tile([P, TILES, HEAD], BF16)
+        sin_sb = keep.tile([P, TILES, HEAD], BF16)
+        table = keep.tile([P, TILES, 2, HEAD], BF16)
+        identity = keep.tile([P, P], F32)
+        x_codes = keep.tile([P, TILES, PASSES * P], U32, align_bytes=64)
+        x_scales = keep.tile([P, TILES, PASSES * P], U8, align_bytes=64)
+        w_codes = keep.tile([P, PASSES, W_COLS], U32, align_bytes=64)
+        w_scales = keep.tile([P, PASSES, W_COLS], U8, align_bytes=64)
+
+        def load_x(t):
+            nc.sync.dma_start(out=x_sb[:, t, :], in_=x_rows[:, t, :])
+
+        def load_codes(words, first, start, width):
+            source = words.bitcast(I32).rearrange("c p n o -> p c (n o)")
+            nc.sync.dma_start(
+                out=w_codes[:, :, start + first : start + first + width].bitcast(I32),
+                in_=source[:, :, first : first + width],
+            )
+
+        def load_scales(scales, start, width):
+            source = scales.bitcast(I32).rearrange("c s n -> s c n")
+            for quadrant in range(2):
+                for r in range(4):
+                    nc.sync.dma_start(
+                        out=w_scales[32 * quadrant + r : P : 64, :, start : start + width].bitcast(I32),
+                        in_=source[4 * quadrant + r : 16 : 8, :, :],
+                    )
+
+        nc.vector.memset(w_scales[:].bitcast(I32), 0)
+        make_identity(nc, identity[:])
+
+        load_x(0)
+        nc.sync.dma_start(out=cos_sb[:], in_=cos_rows)
+        nc.sync.dma_start(out=sin_sb[:], in_=sin_rows)
+        load_scales(Wq_scales, 0, Q_COLS)
+        load_codes(Wq_words, 0, 0, BANK)
+        load_x(1)
+        load_codes(Wq_words, BANK, 0, BANK)
+        for t in range(2, TILES):
+            load_x(t)
+        load_scales(Wv_scales, V_START, V_COLS)
+        load_scales(Wk_scales, K_START, K_COLS)
+        load_codes(Wq_words, 2 * BANK, 0, 2 * BANK)
+        load_codes(Wv_words, 0, V_START, V_COLS)
+        load_codes(Wk_words, 0, K_START, K_COLS)
+
+        factors = table[:].rearrange("p t e (u j) -> p t e u j", u=2)
+        nc.vector.tensor_copy(out=factors[:, :, 0, 0, :], in_=cos_sb[:, :, 0:HALF])
+        nc.vector.tensor_scalar_mul(out=factors[:, :, 0, 1, :], in0=sin_sb[:, :, 0:HALF], scalar1=-1.0)
+        nc.vector.tensor_copy(out=factors[:, :, 1, 0, :], in_=sin_sb[:, :, HALF:HEAD])
+        nc.vector.tensor_copy(out=factors[:, :, 1, 1, :], in_=cos_sb[:, :, HALF:HEAD])
+
+        x_words = x_sb[:].bitcast(F32)
+
+        def quantise_x(t):
+            planes = turned.tile([P, PASSES * 2, P], F32)
+            for c in range(PASSES):
+                for u in range(2):
+                    nc.tensor.transpose(
+                        planes[:, 2 * c + u, :],
+                        x_words[:, t, WORDS * c + u : WORDS * (c + 1) : 2],
+                        identity[:],
+                    )
+            grouped = stage.tile([P, PASSES * P * 4], BF16, align_bytes=64)
+            nc.scalar.copy(
+                out=grouped[:].bitcast(F32).rearrange("p (c r u) -> p c r u", c=PASSES, u=2),
+                in_=planes[:].rearrange("p (c u) r -> p c r u", u=2),
+            )
+            nc.vector.quantize_mx(
+                out=x_codes[:, t, :].bitcast(FP8X4), scales=x_scales[:, t, :], in_=grouped[:]
+            )
+
+        def project(bank, t, start):
+            for c in range(PASSES):
+                nc.tensor.matmul_mx(
+                    out=bank[:],
+                    lhsT=x_codes[:, t, c * P : (c + 1) * P].bitcast(FP8X4),
+                    lhsT_scale=x_scales[:, t, c * P : (c + 1) * P],
+                    rhs=w_codes[:, c, start : start + BANK].bitcast(FP8X4),
+                    rhs_scale=w_scales[:, c, start : start + BANK],
+                    start=(c == 0),
+                    stop=(c == PASSES - 1),
+                )
+
+        def multiply(products, slot, t, start):
+            bank = sums.tile([P, BANK], F32)
+            project(bank, t, start)
+            shape = [P, 2, BANK_HEADS, HEAD]
+            nc.vector.tensor_tensor(
+                out=products[:, :, slot * BANK_HEADS : (slot + 1) * BANK_HEADS, :],
+                in0=bank[:].rearrange("p (h d) -> p h d", d=HEAD).unsqueeze(1).to_broadcast(shape),
+                in1=table[:, t].unsqueeze(2).to_broadcast(shape),
+                op=MULT,
+            )
+
+        def add(products):
+            rotated = stage.tile([P, PAIR * BANK_HEADS, 2, HALF], F32)
+            nc.gpsimd.tensor_tensor(
+                out=rotated[:],
+                in0=products[:, :, :, 0:HALF].rearrange("p e h j -> p h e j"),
+                in1=products[:, :, :, HALF:HEAD].rearrange("p e h j -> p h e j"),
+                op=ADD,
+            )
+            return rotated
+
+        quantise_x(0)
+        for sweep in range(Q_COLS // (PAIR * BANK)):
+            first = sweep * PAIR * BANK
+            for t in range(TILES):
+                products = stage.tile([P, 2, PAIR * BANK_HEADS, HEAD], F32)
+                multiply(products, 0, t, first)
+                if sweep == 0 and t + 1 < TILES:
+                    quantise_x(t + 1)
+                multiply(products, 1, t, first + BANK)
+                rotated = add(products)
+                nc.sync.dma_start(
+                    out=q_rows[:, t, first : first + PAIR * BANK],
+                    in_=rotated[:].rearrange("p h e j -> p (h e j)"),
+                )
+                if sweep == 1 and t % PAIR == PAIR - 1:
+                    v_out = stage.tile([P, PAIR, V_COLS], F32)
+                    for i in range(PAIR):
+                        v_bank = v_sums.tile([P, BANK], F32)
+                        project(v_bank, t + 1 - PAIR + i, V_START)
+                        nc.scalar.copy(out=v_out[:, i, :], in_=v_bank[:])
+                    nc.sync.dma_start(out=v_rows[:, t + 1 - PAIR : t + 1, :], in_=v_out[:])
+
+        for t in range(0, TILES, PAIR):
+            products = stage.tile([P, 2, PAIR * BANK_HEADS, HEAD], F32)
+            for i in range(PAIR):
+                multiply(products, i, t + i, K_START)
+            rotated = add(products)
+            nc.sync.dma_start(
+                out=k_rows[:, t : t + PAIR, :],
+                in_=rotated[:].rearrange("p (i h) e j -> p i (h e j)", i=PAIR),
+            )

@@ -24,14 +24,11 @@ HALF = HEAD // 2
 BANK = 512
 BANK_HEADS = BANK // HEAD
 PAIR = 2
-Q_COLS = 2048
-K_COLS = 512
-V_COLS = 512
-K_START = Q_COLS
-V_START = Q_COLS + K_COLS
-W_COLS = Q_COLS + K_COLS + V_COLS
+VECTOR_EVERY = 10
+Q_BLOCKS = 4
+QUADRANTS = 4
 
-FLOPS = 2 * TOKENS * HIDDEN * W_COLS
+FLOPS = 2 * TOKENS * HIDDEN * (Q_BLOCKS + 2) * BANK
 
 
 def tile_attention_pa_kernel(
@@ -57,55 +54,50 @@ def tile_attention_pa_kernel(
         x_sb = keep.tile([P, TILES, HIDDEN], BF16)
         cos_sb = keep.tile([P, TILES, HEAD], BF16)
         sin_sb = keep.tile([P, TILES, HEAD], BF16)
-        table = keep.tile([P, TILES, 2, HEAD], BF16)
+        factor = keep.tile([P, 2, 2, TILES, HALF], BF16)
         identity = keep.tile([P, P], F32)
         x_codes = keep.tile([P, TILES, PASSES * P], U32, align_bytes=64)
         x_scales = keep.tile([P, TILES, PASSES * P], U8, align_bytes=64)
-        w_codes = keep.tile([P, PASSES, W_COLS], U32, align_bytes=64)
-        w_scales = keep.tile([P, PASSES, W_COLS], U8, align_bytes=64)
+        q_codes = keep.tile([P, Q_BLOCKS, PASSES, BANK], U32, align_bytes=64)
+        k_codes = keep.tile([P, 1, PASSES, BANK], U32, align_bytes=64)
+        v_codes = keep.tile([P, 1, PASSES, BANK], U32, align_bytes=64)
+        q_scales = keep.tile([P, PASSES, Q_BLOCKS * BANK], U8, align_bytes=64)
+        k_scales = keep.tile([P, PASSES, BANK], U8, align_bytes=64)
+        v_scales = keep.tile([P, PASSES, BANK], U8, align_bytes=64)
 
         def load_x(t):
-            nc.sync.dma_start(out=x_sb[:, t, :], in_=x_rows[:, t, :])
+            nc.sync.dma_start(out=x_sb[:, t : t + PAIR, :], in_=x_rows[:, t : t + PAIR, :])
 
-        def load_codes(words, first, start, width):
+        def load_codes(codes, words, block):
             source = words.bitcast(I32).rearrange("c p n o -> p c (n o)")
             nc.sync.dma_start(
-                out=w_codes[:, :, start + first : start + first + width].bitcast(I32),
-                in_=source[:, :, first : first + width],
+                out=codes[:, block].bitcast(I32), in_=source[:, :, block * BANK : (block + 1) * BANK]
             )
 
-        def load_scales(scales, start, width):
+        def load_scales(plane, scales):
+            nc.vector.memset(plane[:].bitcast(I32), 0)
             source = scales.bitcast(I32).rearrange("c s n -> s c n")
-            for quadrant in range(2):
-                for r in range(4):
-                    nc.sync.dma_start(
-                        out=w_scales[32 * quadrant + r : P : 64, :, start : start + width].bitcast(I32),
-                        in_=source[4 * quadrant + r : 16 : 8, :, :],
-                    )
+            for quadrant in range(QUADRANTS):
+                nc.sync.dma_start(
+                    out=plane[32 * quadrant : 32 * quadrant + 4].bitcast(I32),
+                    in_=source[4 * quadrant : 4 * quadrant + 4],
+                )
 
-        nc.vector.memset(w_scales[:].bitcast(I32), 0)
         make_identity(nc, identity[:])
-
         load_x(0)
         nc.sync.dma_start(out=cos_sb[:], in_=cos_rows)
         nc.sync.dma_start(out=sin_sb[:], in_=sin_rows)
-        load_scales(Wq_scales, 0, Q_COLS)
-        load_codes(Wq_words, 0, 0, BANK)
-        load_x(1)
-        load_codes(Wq_words, BANK, 0, BANK)
-        for t in range(2, TILES):
+        load_scales(q_scales, Wq_scales)
+        load_codes(q_codes, Wq_words, 0)
+        load_codes(q_codes, Wq_words, 1)
+        for t in range(PAIR, TILES, PAIR):
             load_x(t)
-        load_scales(Wv_scales, V_START, V_COLS)
-        load_scales(Wk_scales, K_START, K_COLS)
-        load_codes(Wq_words, 2 * BANK, 0, 2 * BANK)
-        load_codes(Wv_words, 0, V_START, V_COLS)
-        load_codes(Wk_words, 0, K_START, K_COLS)
-
-        factors = table[:].rearrange("p t e (u j) -> p t e u j", u=2)
-        nc.vector.tensor_copy(out=factors[:, :, 0, 0, :], in_=cos_sb[:, :, 0:HALF])
-        nc.vector.tensor_scalar_mul(out=factors[:, :, 0, 1, :], in0=sin_sb[:, :, 0:HALF], scalar1=-1.0)
-        nc.vector.tensor_copy(out=factors[:, :, 1, 0, :], in_=sin_sb[:, :, HALF:HEAD])
-        nc.vector.tensor_copy(out=factors[:, :, 1, 1, :], in_=cos_sb[:, :, HALF:HEAD])
+        load_scales(v_scales, Wv_scales)
+        load_scales(k_scales, Wk_scales)
+        load_codes(q_codes, Wq_words, 2)
+        load_codes(q_codes, Wq_words, 3)
+        load_codes(v_codes, Wv_words, 0)
+        load_codes(k_codes, Wk_words, 0)
 
         x_words = x_sb[:].bitcast(F32)
 
@@ -127,67 +119,71 @@ def tile_attention_pa_kernel(
                 out=x_codes[:, t, :].bitcast(FP8X4), scales=x_scales[:, t, :], in_=grouped[:]
             )
 
-        def project(bank, t, start):
+        def project(bank, t, codes, plane, block):
             for c in range(PASSES):
                 nc.tensor.matmul_mx(
                     out=bank[:],
                     lhsT=x_codes[:, t, c * P : (c + 1) * P].bitcast(FP8X4),
                     lhsT_scale=x_scales[:, t, c * P : (c + 1) * P],
-                    rhs=w_codes[:, c, start : start + BANK].bitcast(FP8X4),
-                    rhs_scale=w_scales[:, c, start : start + BANK],
+                    rhs=codes[:, block, c, :].bitcast(FP8X4),
+                    rhs_scale=plane[:, c, block * BANK : (block + 1) * BANK],
                     start=(c == 0),
                     stop=(c == PASSES - 1),
                 )
 
-        def multiply(products, slot, t, start):
+        def multiply(products, slot, t, codes, plane, block):
             bank = sums.tile([P, BANK], F32)
-            project(bank, t, start)
-            shape = [P, 2, BANK_HEADS, HEAD]
+            project(bank, t, codes, plane, block)
             nc.vector.tensor_tensor(
-                out=products[:, :, slot * BANK_HEADS : (slot + 1) * BANK_HEADS, :],
-                in0=bank[:].rearrange("p (h d) -> p h d", d=HEAD).unsqueeze(1).to_broadcast(shape),
-                in1=table[:, t].unsqueeze(2).to_broadcast(shape),
+                out=products[:, slot].rearrange("p h e (u j) -> p h e u j", u=2),
+                in0=bank[:]
+                .rearrange("p (h u j) -> p h u j", u=2, j=HALF)
+                .unsqueeze(2)
+                .to_broadcast([P, BANK_HEADS, 2, 2, HALF]),
+                in1=factor[:, :, :, t, :].unsqueeze(1).to_broadcast([P, BANK_HEADS, 2, 2, HALF]),
                 op=MULT,
             )
 
-        def add(products):
-            rotated = stage.tile([P, PAIR * BANK_HEADS, 2, HALF], F32)
-            nc.gpsimd.tensor_tensor(
-                out=rotated[:],
-                in0=products[:, :, :, 0:HALF].rearrange("p e h j -> p h e j"),
-                in1=products[:, :, :, HALF:HEAD].rearrange("p e h j -> p h e j"),
-                op=ADD,
-            )
+        def add(products, count):
+            rotated = stage.tile([P, PAIR * BANK_HEADS * 2, HALF], F32)
+            halves = products[:].rearrange("p s h e (u j) -> p (s h e) u j", u=2)
+            engine = nc.vector if count % VECTOR_EVERY == VECTOR_EVERY - 1 else nc.gpsimd
+            engine.tensor_tensor(out=rotated[:], in0=halves[:, :, 0, :], in1=halves[:, :, 1, :], op=ADD)
             return rotated
 
         quantise_x(0)
-        for sweep in range(Q_COLS // (PAIR * BANK)):
-            first = sweep * PAIR * BANK
+
+        nc.vector.tensor_copy(out=factor[:, 0, 0], in_=cos_sb[:, :, 0:HALF])
+        nc.vector.tensor_scalar_mul(out=factor[:, 0, 1], in0=sin_sb[:, :, 0:HALF], scalar1=-1.0)
+        nc.vector.tensor_copy(out=factor[:, 1, 0], in_=sin_sb[:, :, HALF:HEAD])
+        nc.vector.tensor_copy(out=factor[:, 1, 1], in_=cos_sb[:, :, HALF:HEAD])
+
+        for sweep in range(Q_BLOCKS // PAIR):
             for t in range(TILES):
-                products = stage.tile([P, 2, PAIR * BANK_HEADS, HEAD], F32)
-                multiply(products, 0, t, first)
+                products = stage.tile([P, PAIR, BANK_HEADS, 2, HEAD], F32)
+                multiply(products, 0, t, q_codes, q_scales, sweep * PAIR)
                 if sweep == 0 and t + 1 < TILES:
                     quantise_x(t + 1)
-                multiply(products, 1, t, first + BANK)
-                rotated = add(products)
+                multiply(products, 1, t, q_codes, q_scales, sweep * PAIR + 1)
+                rotated = add(products, sweep * TILES + t)
                 nc.sync.dma_start(
-                    out=q_rows[:, t, first : first + PAIR * BANK],
-                    in_=rotated[:].rearrange("p h e j -> p (h e j)"),
+                    out=q_rows[:, t, sweep * PAIR * BANK : (sweep + 1) * PAIR * BANK],
+                    in_=rotated[:].rearrange("p g j -> p (g j)"),
                 )
                 if sweep == 1 and t % PAIR == PAIR - 1:
-                    v_out = stage.tile([P, PAIR, V_COLS], F32)
+                    v_out = stage.tile([P, PAIR, BANK], F32)
                     for i in range(PAIR):
                         v_bank = v_sums.tile([P, BANK], F32)
-                        project(v_bank, t + 1 - PAIR + i, V_START)
+                        project(v_bank, t + 1 - PAIR + i, v_codes, v_scales, 0)
                         nc.scalar.copy(out=v_out[:, i, :], in_=v_bank[:])
                     nc.sync.dma_start(out=v_rows[:, t + 1 - PAIR : t + 1, :], in_=v_out[:])
 
         for t in range(0, TILES, PAIR):
-            products = stage.tile([P, 2, PAIR * BANK_HEADS, HEAD], F32)
+            products = stage.tile([P, PAIR, BANK_HEADS, 2, HEAD], F32)
             for i in range(PAIR):
-                multiply(products, i, t + i, K_START)
-            rotated = add(products)
+                multiply(products, i, t + i, k_codes, k_scales, 0)
+            rotated = add(products, Q_BLOCKS // PAIR * TILES + t // PAIR)
             nc.sync.dma_start(
                 out=k_rows[:, t : t + PAIR, :],
-                in_=rotated[:].rearrange("p (i h) e j -> p i (h e j)", i=PAIR),
+                in_=rotated[:].rearrange("p (i g) j -> p i (g j)", i=PAIR),
             )

@@ -24,7 +24,7 @@ HALF = HEAD // 2
 BANK = 512
 BANK_HEADS = BANK // HEAD
 PAIR = 2
-VECTOR_EVERY = 10
+EARLY = 3
 Q_BLOCKS = 4
 QUADRANTS = 4
 
@@ -46,6 +46,7 @@ def tile_attention_pa_kernel(
     with ExitStack() as ctx:
         keep = ctx.enter_context(tc.tile_pool(name="keep", bufs=1))
         stage = ctx.enter_context(tc.tile_pool(name="stage", bufs=3))
+        wide = ctx.enter_context(tc.tile_pool(name="wide", bufs=EARLY + 2))
         turned = ctx.enter_context(tc.psum_pool(name="turned", bufs=2))
         sums = ctx.enter_context(tc.psum_pool(name="sums", bufs=4))
         v_sums = ctx.enter_context(tc.psum_pool(name="v_sums", bufs=2))
@@ -65,8 +66,8 @@ def tile_attention_pa_kernel(
         k_scales = keep.tile([P, PASSES, BANK], U8, align_bytes=64)
         v_scales = keep.tile([P, PASSES, BANK], U8, align_bytes=64)
 
-        def load_x(t):
-            nc.sync.dma_start(out=x_sb[:, t : t + PAIR, :], in_=x_rows[:, t : t + PAIR, :])
+        def load_x(t, count):
+            nc.sync.dma_start(out=x_sb[:, t : t + count, :], in_=x_rows[:, t : t + count, :])
 
         def load_codes(codes, words, block):
             source = words.bitcast(I32).rearrange("c p n o -> p c (n o)")
@@ -84,14 +85,15 @@ def tile_attention_pa_kernel(
                 )
 
         make_identity(nc, identity[:])
-        load_x(0)
+        load_x(0, 1)
+        load_scales(q_scales, Wq_scales)
         nc.sync.dma_start(out=cos_sb[:], in_=cos_rows)
         nc.sync.dma_start(out=sin_sb[:], in_=sin_rows)
-        load_scales(q_scales, Wq_scales)
         load_codes(q_codes, Wq_words, 0)
-        load_codes(q_codes, Wq_words, 1)
+        load_x(1, 1)
         for t in range(PAIR, TILES, PAIR):
-            load_x(t)
+            load_x(t, PAIR)
+        load_codes(q_codes, Wq_words, 1)
         load_scales(v_scales, Wv_scales)
         load_scales(k_scales, Wk_scales)
         load_codes(q_codes, Wq_words, 2)
@@ -144,12 +146,15 @@ def tile_attention_pa_kernel(
                 op=MULT,
             )
 
-        def add(products, count):
+        def add(products, engine):
             rotated = stage.tile([P, PAIR * BANK_HEADS * 2, HALF], F32)
             halves = products[:].rearrange("p s h e (u j) -> p (s h e) u j", u=2)
-            engine = nc.vector if count % VECTOR_EVERY == VECTOR_EVERY - 1 else nc.gpsimd
             engine.tensor_tensor(out=rotated[:], in0=halves[:, :, 0, :], in1=halves[:, :, 1, :], op=ADD)
             return rotated
+
+        def new_products():
+            products = wide.tile([P, PAIR, BANK_HEADS, 2, HEAD], F32)
+            return products
 
         quantise_x(0)
 
@@ -158,14 +163,23 @@ def tile_attention_pa_kernel(
         nc.vector.tensor_copy(out=factor[:, 1, 0], in_=sin_sb[:, :, HALF:HEAD])
         nc.vector.tensor_copy(out=factor[:, 1, 1], in_=cos_sb[:, :, HALF:HEAD])
 
+        started = []
+        for t in range(TILES):
+            if t > 0:
+                quantise_x(t)
+            if t < EARLY:
+                started.append(new_products())
+                multiply(started[t], 0, t, q_codes, q_scales, 0)
+
         for sweep in range(Q_BLOCKS // PAIR):
             for t in range(TILES):
-                products = stage.tile([P, PAIR, BANK_HEADS, 2, HEAD], F32)
-                multiply(products, 0, t, q_codes, q_scales, sweep * PAIR)
-                if sweep == 0 and t + 1 < TILES:
-                    quantise_x(t + 1)
+                if sweep == 0 and t < EARLY:
+                    products = started[t]
+                else:
+                    products = new_products()
+                    multiply(products, 0, t, q_codes, q_scales, sweep * PAIR)
                 multiply(products, 1, t, q_codes, q_scales, sweep * PAIR + 1)
-                rotated = add(products, sweep * TILES + t)
+                rotated = add(products, nc.gpsimd)
                 nc.sync.dma_start(
                     out=q_rows[:, t, sweep * PAIR * BANK : (sweep + 1) * PAIR * BANK],
                     in_=rotated[:].rearrange("p g j -> p (g j)"),
@@ -179,10 +193,10 @@ def tile_attention_pa_kernel(
                     nc.sync.dma_start(out=v_rows[:, t + 1 - PAIR : t + 1, :], in_=v_out[:])
 
         for t in range(0, TILES, PAIR):
-            products = stage.tile([P, PAIR, BANK_HEADS, 2, HEAD], F32)
+            products = new_products()
             for i in range(PAIR):
                 multiply(products, i, t + i, k_codes, k_scales, 0)
-            rotated = add(products, Q_BLOCKS // PAIR * TILES + t // PAIR)
+            rotated = add(products, nc.vector if t + PAIR == TILES else nc.gpsimd)
             nc.sync.dma_start(
                 out=k_rows[:, t : t + PAIR, :],
                 in_=rotated[:].rearrange("p (i g) j -> p i (g j)", i=PAIR),

@@ -192,11 +192,14 @@ def tile_attention_pa_kernel(
                         nc.scalar.copy(out=v_out[:, i, :], in_=v_bank[:])
                     nc.sync.dma_start(out=v_rows[:, t + 1 - PAIR : t + 1, :], in_=v_out[:])
 
+        k_products = []
         for t in range(0, TILES, PAIR):
             products = new_products()
             for i in range(PAIR):
                 multiply(products, i, t + i, k_codes, k_scales, 0)
-            rotated = add(products, nc.vector if t + PAIR == TILES else nc.gpsimd)
+            k_products.append(products)
+        for t in range(0, TILES, PAIR):
+            rotated = add(k_products[t // PAIR], nc.vector)
             nc.sync.dma_start(
                 out=k_rows[:, t : t + PAIR, :],
                 in_=rotated[:].rearrange("p (i g) j -> p i (g j)", i=PAIR),

@@ -24,7 +24,6 @@ HALF = HEAD // 2
 BANK = 512
 BANK_HEADS = BANK // HEAD
 PAIR = 2
-EARLY = 3
 Q_BLOCKS = 4
 QUADRANTS = 4
 
@@ -46,7 +45,7 @@ def tile_attention_pa_kernel(
     with ExitStack() as ctx:
         keep = ctx.enter_context(tc.tile_pool(name="keep", bufs=1))
         stage = ctx.enter_context(tc.tile_pool(name="stage", bufs=3))
-        wide = ctx.enter_context(tc.tile_pool(name="wide", bufs=EARLY + 2))
+        wide = ctx.enter_context(tc.tile_pool(name="wide", bufs=10))
         turned = ctx.enter_context(tc.psum_pool(name="turned", bufs=2))
         sums = ctx.enter_context(tc.psum_pool(name="sums", bufs=4))
         v_sums = ctx.enter_context(tc.psum_pool(name="v_sums", bufs=2))
@@ -86,18 +85,18 @@ def tile_attention_pa_kernel(
 
         make_identity(nc, identity[:])
         load_x(0, 1)
-        load_scales(q_scales, Wq_scales)
-        nc.sync.dma_start(out=cos_sb[:], in_=cos_rows)
-        nc.sync.dma_start(out=sin_sb[:], in_=sin_rows)
-        load_codes(q_codes, Wq_words, 0)
         load_x(1, 1)
         for t in range(PAIR, TILES, PAIR):
             load_x(t, PAIR)
+        nc.sync.dma_start(out=cos_sb[:], in_=cos_rows)
+        nc.sync.dma_start(out=sin_sb[:], in_=sin_rows)
+        load_codes(q_codes, Wq_words, 0)
+        load_scales(q_scales, Wq_scales)
         load_codes(q_codes, Wq_words, 1)
-        load_scales(v_scales, Wv_scales)
-        load_scales(k_scales, Wk_scales)
         load_codes(q_codes, Wq_words, 2)
         load_codes(q_codes, Wq_words, 3)
+        load_scales(v_scales, Wv_scales)
+        load_scales(k_scales, Wk_scales)
         load_codes(v_codes, Wv_words, 0)
         load_codes(k_codes, Wk_words, 0)
 
@@ -113,7 +112,8 @@ def tile_attention_pa_kernel(
                         identity[:],
                     )
             grouped = stage.tile([P, PASSES * P * 4], BF16, align_bytes=64)
-            nc.scalar.copy(
+            copy = nc.scalar.copy if t % 2 == 0 else nc.vector.tensor_copy
+            copy(
                 out=grouped[:].bitcast(F32).rearrange("p (c r u) -> p c r u", c=PASSES, u=2),
                 in_=planes[:].rearrange("p (c u) r -> p c r u", u=2),
             )
@@ -152,32 +152,30 @@ def tile_attention_pa_kernel(
             engine.tensor_tensor(out=rotated[:], in0=halves[:, :, 0, :], in1=halves[:, :, 1, :], op=ADD)
             return rotated
 
+        def add_bank(products, slot):
+            rotated_bank = stage.tile([P, BANK_HEADS * 2, HALF], F32)
+            halves = products[:, slot].rearrange("p h e (u j) -> p (h e) u j", u=2)
+            nc.vector.tensor_tensor(
+                out=rotated_bank[:], in0=halves[:, :, 0, :], in1=halves[:, :, 1, :], op=ADD
+            )
+            return rotated_bank
+
         def new_products():
             products = wide.tile([P, PAIR, BANK_HEADS, 2, HEAD], F32)
             return products
 
-        quantise_x(0)
+        for t in range(TILES):
+            quantise_x(t)
 
         nc.vector.tensor_copy(out=factor[:, 0, 0], in_=cos_sb[:, :, 0:HALF])
         nc.vector.tensor_scalar_mul(out=factor[:, 0, 1], in0=sin_sb[:, :, 0:HALF], scalar1=-1.0)
         nc.vector.tensor_copy(out=factor[:, 1, 0], in_=sin_sb[:, :, HALF:HEAD])
         nc.vector.tensor_copy(out=factor[:, 1, 1], in_=cos_sb[:, :, HALF:HEAD])
 
-        started = []
-        for t in range(TILES):
-            if t > 0:
-                quantise_x(t)
-            if t < EARLY:
-                started.append(new_products())
-                multiply(started[t], 0, t, q_codes, q_scales, 0)
-
         for sweep in range(Q_BLOCKS // PAIR):
             for t in range(TILES):
-                if sweep == 0 and t < EARLY:
-                    products = started[t]
-                else:
-                    products = new_products()
-                    multiply(products, 0, t, q_codes, q_scales, sweep * PAIR)
+                products = new_products()
+                multiply(products, 0, t, q_codes, q_scales, sweep * PAIR)
                 multiply(products, 1, t, q_codes, q_scales, sweep * PAIR + 1)
                 rotated = add(products, nc.gpsimd)
                 nc.sync.dma_start(
@@ -197,10 +195,13 @@ def tile_attention_pa_kernel(
             products = new_products()
             for i in range(PAIR):
                 multiply(products, i, t + i, k_codes, k_scales, 0)
+            if t == 0:
+                rotated = add(products, nc.gpsimd)
+                nc.sync.dma_start(
+                    out=k_rows[:, t : t + PAIR, :],
+                    in_=rotated[:].rearrange("p (i g) j -> p i (g j)", i=PAIR),
+                )
             k_products.append(products)
-        for t in range(0, TILES, PAIR):
-            rotated = add(k_products[t // PAIR], nc.vector)
-            nc.sync.dma_start(
-                out=k_rows[:, t : t + PAIR, :],
-                in_=rotated[:].rearrange("p (i g) j -> p i (g j)", i=PAIR),
-            )
+        for t in range(PAIR, TILES):
+            rotated_bank = add_bank(k_products[t // PAIR], t % PAIR)
+            nc.sync.dma_start(out=k_rows[:, t, :], in_=rotated_bank[:].rearrange("p g j -> p (g j)"))

@@ -24,6 +24,7 @@ HALF = HEAD // 2
 BANK = 512
 BANK_HEADS = BANK // HEAD
 PAIR = 2
+EARLY = 2
 Q_BLOCKS = 4
 QUADRANTS = 4
 
@@ -46,6 +47,7 @@ def tile_attention_pa_kernel(
         keep = ctx.enter_context(tc.tile_pool(name="keep", bufs=1))
         stage = ctx.enter_context(tc.tile_pool(name="stage", bufs=3))
         wide = ctx.enter_context(tc.tile_pool(name="wide", bufs=10))
+        upright = ctx.enter_context(tc.tile_pool(name="upright", bufs=3))
         turned = ctx.enter_context(tc.psum_pool(name="turned", bufs=2))
         sums = ctx.enter_context(tc.psum_pool(name="sums", bufs=4))
         v_sums = ctx.enter_context(tc.psum_pool(name="v_sums", bufs=2))
@@ -56,8 +58,12 @@ def tile_attention_pa_kernel(
         sin_sb = keep.tile([P, TILES, HEAD], BF16)
         factor = keep.tile([P, 2, 2, TILES, HALF], BF16)
         identity = keep.tile([P, P], F32)
-        x_codes = keep.tile([P, TILES, PASSES * P], U32, align_bytes=64)
-        x_scales = keep.tile([P, TILES, PASSES * P], U8, align_bytes=64)
+        swap = keep.tile([P, P], F32)
+        identity_bf = keep.tile([P, P], BF16)
+        partner_sin = keep.tile([P, TILES, HEAD], BF16)
+        tables = keep.tile([P, 2, TOKENS], BF16)
+        x_codes = keep.tile([P, PASSES, TOKENS], U32, align_bytes=64)
+        x_scales = keep.tile([P, PASSES, TOKENS], U8, align_bytes=64)
         q_codes = keep.tile([P, Q_BLOCKS, PASSES, BANK], U32, align_bytes=64)
         k_codes = keep.tile([P, 1, PASSES, BANK], U32, align_bytes=64)
         v_codes = keep.tile([P, 1, PASSES, BANK], U32, align_bytes=64)
@@ -84,21 +90,25 @@ def tile_attention_pa_kernel(
                 )
 
         make_identity(nc, identity[:])
+        make_identity(nc, identity_bf[:])
         load_x(0, 1)
         load_x(1, 1)
-        for t in range(PAIR, TILES, PAIR):
-            load_x(t, PAIR)
+        load_x(2, PAIR)
         nc.sync.dma_start(out=cos_sb[:], in_=cos_rows)
         nc.sync.dma_start(out=sin_sb[:], in_=sin_rows)
+        load_x(4, PAIR)
         load_codes(q_codes, Wq_words, 0)
         load_scales(q_scales, Wq_scales)
+        load_x(6, PAIR)
         load_codes(q_codes, Wq_words, 1)
+        load_scales(v_scales, Wv_scales)
+        load_codes(v_codes, Wv_words, 0)
+        load_scales(k_scales, Wk_scales)
+        load_codes(k_codes, Wk_words, 0)
         load_codes(q_codes, Wq_words, 2)
         load_codes(q_codes, Wq_words, 3)
-        load_scales(v_scales, Wv_scales)
-        load_scales(k_scales, Wk_scales)
-        load_codes(v_codes, Wv_words, 0)
-        load_codes(k_codes, Wk_words, 0)
+        nc.vector.tensor_copy(out=swap[:, 0:HALF], in_=identity[:, HALF:P])
+        nc.vector.tensor_copy(out=swap[:, HALF:P], in_=identity[:, 0:HALF])
 
         x_words = x_sb[:].bitcast(F32)
 
@@ -112,21 +122,24 @@ def tile_attention_pa_kernel(
                         identity[:],
                     )
             grouped = stage.tile([P, PASSES * P * 4], BF16, align_bytes=64)
-            copy = nc.scalar.copy if t % 2 == 0 else nc.vector.tensor_copy
+            copy = nc.vector.tensor_copy if t in (1, 3, 5) else nc.scalar.copy
             copy(
                 out=grouped[:].bitcast(F32).rearrange("p (c r u) -> p c r u", c=PASSES, u=2),
                 in_=planes[:].rearrange("p (c u) r -> p c r u", u=2),
             )
-            nc.vector.quantize_mx(
-                out=x_codes[:, t, :].bitcast(FP8X4), scales=x_scales[:, t, :], in_=grouped[:]
-            )
+            for c in range(PASSES):
+                nc.vector.quantize_mx(
+                    out=x_codes[:, c, t * P : (t + 1) * P].bitcast(FP8X4),
+                    scales=x_scales[:, c, t * P : (t + 1) * P],
+                    in_=grouped[:, c * K_PASS : (c + 1) * K_PASS],
+                )
 
         def project(bank, t, codes, plane, block):
             for c in range(PASSES):
                 nc.tensor.matmul_mx(
                     out=bank[:],
-                    lhsT=x_codes[:, t, c * P : (c + 1) * P].bitcast(FP8X4),
-                    lhsT_scale=x_scales[:, t, c * P : (c + 1) * P],
+                    lhsT=x_codes[:, c, t * P : (t + 1) * P].bitcast(FP8X4),
+                    lhsT_scale=x_scales[:, c, t * P : (t + 1) * P],
                     rhs=codes[:, block, c, :].bitcast(FP8X4),
                     rhs_scale=plane[:, c, block * BANK : (block + 1) * BANK],
                     start=(c == 0),
@@ -160,11 +173,57 @@ def tile_attention_pa_kernel(
             )
             return rotated_bank
 
+        def turn_table(which, rows):
+            planes = turned.tile([P, TILES, P], BF16)
+            for t in range(TILES):
+                nc.tensor.transpose(planes[:, t, :], rows[:, t, :], identity_bf[:])
+            nc.scalar.copy(out=tables[:, which, :], in_=planes[:].rearrange("p t r -> p (t r)"))
+
+        def multiply_upright(group, head):
+            bank = sums.tile([P, BANK], F32)
+            tokens = slice(group * BANK, (group + 1) * BANK)
+            for c in range(PASSES):
+                nc.tensor.matmul_mx(
+                    out=bank[:],
+                    lhsT=k_codes[:, 0, c, head * P : (head + 1) * P].bitcast(FP8X4),
+                    lhsT_scale=k_scales[:, c, head * P : (head + 1) * P],
+                    rhs=x_codes[:, c, tokens].bitcast(FP8X4),
+                    rhs_scale=x_scales[:, c, tokens],
+                    start=(c == 0),
+                    stop=(c == PASSES - 1),
+                )
+            both = upright.tile([P, 2, BANK], F32)
+            nc.vector.tensor_tensor(
+                out=both[:],
+                in0=bank[:].unsqueeze(1).to_broadcast([P, 2, BANK]),
+                in1=tables[:, :, tokens],
+                op=MULT,
+            )
+            return both
+
+        def lay_down(both, group, head):
+            planes = turned.tile([P, BANK_HEADS, P], F32)
+            for i in range(BANK_HEADS):
+                nc.tensor.matmul(
+                    out=planes[:, i, :], lhsT=both[:, 0, i * P : (i + 1) * P], rhs=identity[:],
+                    is_transpose=True, start=True, stop=False,
+                )
+                nc.tensor.matmul(
+                    out=planes[:, i, :], lhsT=both[:, 1, i * P : (i + 1) * P], rhs=swap[:],
+                    is_transpose=True, start=False, stop=True,
+                )
+            k_part = stage.tile([P, BANK_HEADS, P], F32)
+            nc.scalar.copy(out=k_part[:], in_=planes[:])
+            nc.sync.dma_start(
+                out=k_rows[:, group * BANK_HEADS : (group + 1) * BANK_HEADS, head * P : (head + 1) * P],
+                in_=k_part[:],
+            )
+
         def new_products():
             products = wide.tile([P, PAIR, BANK_HEADS, 2, HEAD], F32)
             return products
 
-        for t in range(TILES):
+        for t in range(4):
             quantise_x(t)
 
         nc.vector.tensor_copy(out=factor[:, 0, 0], in_=cos_sb[:, :, 0:HALF])
@@ -172,36 +231,49 @@ def tile_attention_pa_kernel(
         nc.vector.tensor_copy(out=factor[:, 1, 0], in_=sin_sb[:, :, HALF:HEAD])
         nc.vector.tensor_copy(out=factor[:, 1, 1], in_=cos_sb[:, :, HALF:HEAD])
 
+        for t in range(4, 6):
+            quantise_x(t)
+        started = []
+        for t in range(EARLY):
+            started.append(new_products())
+            multiply(started[t], 0, t, q_codes, q_scales, 0)
+        for t in range(6, TILES):
+            quantise_x(t)
+
+        nc.scalar.copy(out=partner_sin[:, :, 0:HALF], in_=sin_sb[:, :, HALF:HEAD])
+        nc.scalar.mul(out=partner_sin[:, :, HALF:HEAD], in_=sin_sb[:, :, 0:HALF], mul=-1.0)
+
         for sweep in range(Q_BLOCKS // PAIR):
             for t in range(TILES):
-                products = new_products()
-                multiply(products, 0, t, q_codes, q_scales, sweep * PAIR)
+                if sweep == 1:
+                    both = multiply_upright(t // BANK_HEADS, t % BANK_HEADS)
+                if sweep == 0 and t < EARLY:
+                    products = started[t]
+                else:
+                    products = new_products()
+                    multiply(products, 0, t, q_codes, q_scales, sweep * PAIR)
                 multiply(products, 1, t, q_codes, q_scales, sweep * PAIR + 1)
-                rotated = add(products, nc.gpsimd)
-                nc.sync.dma_start(
-                    out=q_rows[:, t, sweep * PAIR * BANK : (sweep + 1) * PAIR * BANK],
-                    in_=rotated[:].rearrange("p g j -> p (g j)"),
-                )
-                if sweep == 1 and t % PAIR == PAIR - 1:
+                if sweep == 1:
+                    lay_down(both, t // BANK_HEADS, t % BANK_HEADS)
+                columns = slice(sweep * PAIR * BANK, (sweep + 1) * PAIR * BANK)
+                if sweep == 1 and t == TILES - 1:
+                    for i in range(PAIR):
+                        rotated_bank = add_bank(products, i)
+                        nc.sync.dma_start(
+                            out=q_rows[:, t, columns.start + i * BANK : columns.start + (i + 1) * BANK],
+                            in_=rotated_bank[:].rearrange("p g j -> p (g j)"),
+                        )
+                else:
+                    rotated = add(products, nc.gpsimd)
+                    nc.sync.dma_start(out=q_rows[:, t, columns], in_=rotated[:].rearrange("p g j -> p (g j)"))
+                if sweep == 0 and t % PAIR == PAIR - 1:
                     v_out = stage.tile([P, PAIR, BANK], F32)
                     for i in range(PAIR):
                         v_bank = v_sums.tile([P, BANK], F32)
                         project(v_bank, t + 1 - PAIR + i, v_codes, v_scales, 0)
                         nc.scalar.copy(out=v_out[:, i, :], in_=v_bank[:])
                     nc.sync.dma_start(out=v_rows[:, t + 1 - PAIR : t + 1, :], in_=v_out[:])
-
-        k_products = []
-        for t in range(0, TILES, PAIR):
-            products = new_products()
-            for i in range(PAIR):
-                multiply(products, i, t + i, k_codes, k_scales, 0)
-            if t == 0:
-                rotated = add(products, nc.gpsimd)
-                nc.sync.dma_start(
-                    out=k_rows[:, t : t + PAIR, :],
-                    in_=rotated[:].rearrange("p (i g) j -> p i (g j)", i=PAIR),
-                )
-            k_products.append(products)
-        for t in range(PAIR, TILES):
-            rotated_bank = add_bank(k_products[t // PAIR], t % PAIR)
-            nc.sync.dma_start(out=k_rows[:, t, :], in_=rotated_bank[:].rearrange("p g j -> p (g j)"))
+                if sweep == 0 and t == 2:
+                    turn_table(0, cos_sb)
+                if sweep == 0 and t == 4:
+                    turn_table(1, partner_sin)

@@ -25,6 +25,7 @@ BANK = 512
 BANK_HEADS = BANK // HEAD
 PAIR = 2
 EARLY = 2
+GPSIMD_MULTIPLIES = (1, 4)
 Q_BLOCKS = 4
 QUADRANTS = 4
 
@@ -146,10 +147,16 @@ def tile_attention_pa_kernel(
                     stop=(c == PASSES - 1),
                 )
 
-        def multiply(products, slot, t, codes, plane, block):
+        def multiply(products, slot, t, codes, plane, block, on_gpsimd=False):
             bank = sums.tile([P, BANK], F32)
             project(bank, t, codes, plane, block)
-            nc.vector.tensor_tensor(
+            engine = nc.vector
+            if on_gpsimd:
+                copied = stage.tile([P, BANK], F32)
+                nc.scalar.copy(out=copied[:], in_=bank[:])
+                bank = copied
+                engine = nc.gpsimd
+            engine.tensor_tensor(
                 out=products[:, slot].rearrange("p h e (u j) -> p h e u j", u=2),
                 in0=bank[:]
                 .rearrange("p (h u j) -> p h u j", u=2, j=HALF)
@@ -252,7 +259,10 @@ def tile_attention_pa_kernel(
                 else:
                     products = new_products()
                     multiply(products, 0, t, q_codes, q_scales, sweep * PAIR)
-                multiply(products, 1, t, q_codes, q_scales, sweep * PAIR + 1)
+                multiply(
+                    products, 1, t, q_codes, q_scales, sweep * PAIR + 1,
+                    on_gpsimd=(sweep == 1 and t in GPSIMD_MULTIPLIES),
+                )
                 if sweep == 1:
                     lay_down(both, t // BANK_HEADS, t % BANK_HEADS)
                 columns = slice(sweep * PAIR * BANK, (sweep + 1) * PAIR * BANK)

@@ -25,7 +25,7 @@ BANK = 512
 BANK_HEADS = BANK // HEAD
 PAIR = 2
 EARLY = 2
-GPSIMD_MULTIPLIES = (1, 4)
+GPSIMD_MULTIPLIES = (3,)
 Q_BLOCKS = 4
 QUADRANTS = 4
 

@@ -49,6 +49,7 @@ def tile_attention_pa_kernel(
         stage = ctx.enter_context(tc.tile_pool(name="stage", bufs=3))
         wide = ctx.enter_context(tc.tile_pool(name="wide", bufs=10))
         upright = ctx.enter_context(tc.tile_pool(name="upright", bufs=3))
+        leaving = ctx.enter_context(tc.tile_pool(name="leaving", bufs=6))
         turned = ctx.enter_context(tc.psum_pool(name="turned", bufs=2))
         sums = ctx.enter_context(tc.psum_pool(name="sums", bufs=4))
         v_sums = ctx.enter_context(tc.psum_pool(name="v_sums", bufs=2))
@@ -167,7 +168,7 @@ def tile_attention_pa_kernel(
             )
 
         def add(products, engine):
-            rotated = stage.tile([P, PAIR * BANK_HEADS * 2, HALF], F32)
+            rotated = leaving.tile([P, PAIR * BANK_HEADS * 2, HALF], F32)
             halves = products[:].rearrange("p s h e (u j) -> p (s h e) u j", u=2)
             engine.tensor_tensor(out=rotated[:], in0=halves[:, :, 0, :], in1=halves[:, :, 1, :], op=ADD)
             return rotated
@@ -221,7 +222,7 @@ def tile_attention_pa_kernel(
                 )
             k_part = stage.tile([P, BANK_HEADS, P], F32)
             nc.scalar.copy(out=k_part[:], in_=planes[:])
-            nc.sync.dma_start(
+            nc.scalar.dma_start(
                 out=k_rows[:, group * BANK_HEADS : (group + 1) * BANK_HEADS, head * P : (head + 1) * P],
                 in_=k_part[:],
             )
@@ -250,6 +251,7 @@ def tile_attention_pa_kernel(
         nc.scalar.copy(out=partner_sin[:, :, 0:HALF], in_=sin_sb[:, :, HALF:HEAD])
         nc.scalar.mul(out=partner_sin[:, :, HALF:HEAD], in_=sin_sb[:, :, 0:HALF], mul=-1.0)
 
+        waiting = []
         for sweep in range(Q_BLOCKS // PAIR):
             for t in range(TILES):
                 if sweep == 1:
@@ -259,11 +261,16 @@ def tile_attention_pa_kernel(
                 else:
                     products = new_products()
                     multiply(products, 0, t, q_codes, q_scales, sweep * PAIR)
+                for late in waiting:
+                    lay_down(late, (t - 1) // BANK_HEADS, (t - 1) % BANK_HEADS)
+                waiting = []
                 multiply(
                     products, 1, t, q_codes, q_scales, sweep * PAIR + 1,
                     on_gpsimd=(sweep == 1 and t in GPSIMD_MULTIPLIES),
                 )
                 if sweep == 1:
+                    waiting = [both]
+                if sweep == 1 and t == TILES - 1:
                     lay_down(both, t // BANK_HEADS, t % BANK_HEADS)
                 columns = slice(sweep * PAIR * BANK, (sweep + 1) * PAIR * BANK)
                 if sweep == 1 and t == TILES - 1:
@@ -282,7 +289,7 @@ def tile_attention_pa_kernel(
                         v_bank = v_sums.tile([P, BANK], F32)
                         project(v_bank, t + 1 - PAIR + i, v_codes, v_scales, 0)
                         nc.scalar.copy(out=v_out[:, i, :], in_=v_bank[:])
-                    nc.sync.dma_start(out=v_rows[:, t + 1 - PAIR : t + 1, :], in_=v_out[:])
+                    nc.scalar.dma_start(out=v_rows[:, t + 1 - PAIR : t + 1, :], in_=v_out[:])
                 if sweep == 0 and t == 2:
                     turn_table(0, cos_sb)
                 if sweep == 0 and t == 4:

@@ -24,8 +24,9 @@ HALF = HEAD // 2
 BANK = 512
 BANK_HEADS = BANK // HEAD
 PAIR = 2
-EARLY = 2
-GPSIMD_MULTIPLIES = (3,)
+GROUP = 4
+GPSIMD_MULTIPLIES = ((5, 3),)
+FINE_UNITS = 2
 Q_BLOCKS = 4
 QUADRANTS = 4
 
@@ -47,9 +48,9 @@ def tile_attention_pa_kernel(
     with ExitStack() as ctx:
         keep = ctx.enter_context(tc.tile_pool(name="keep", bufs=1))
         stage = ctx.enter_context(tc.tile_pool(name="stage", bufs=3))
-        wide = ctx.enter_context(tc.tile_pool(name="wide", bufs=10))
+        wide = ctx.enter_context(tc.tile_pool(name="wide", bufs=5))
         upright = ctx.enter_context(tc.tile_pool(name="upright", bufs=3))
-        leaving = ctx.enter_context(tc.tile_pool(name="leaving", bufs=6))
+        leaving = ctx.enter_context(tc.tile_pool(name="leaving", bufs=3))
         turned = ctx.enter_context(tc.psum_pool(name="turned", bufs=2))
         sums = ctx.enter_context(tc.psum_pool(name="sums", bufs=4))
         v_sums = ctx.enter_context(tc.psum_pool(name="v_sums", bufs=2))
@@ -98,13 +99,13 @@ def tile_attention_pa_kernel(
         load_x(2, PAIR)
         nc.sync.dma_start(out=cos_sb[:], in_=cos_rows)
         nc.sync.dma_start(out=sin_sb[:], in_=sin_rows)
-        load_x(4, PAIR)
         load_codes(q_codes, Wq_words, 0)
         load_scales(q_scales, Wq_scales)
+        load_x(4, PAIR)
         load_x(6, PAIR)
-        load_codes(q_codes, Wq_words, 1)
         load_scales(v_scales, Wv_scales)
         load_codes(v_codes, Wv_words, 0)
+        load_codes(q_codes, Wq_words, 1)
         load_scales(k_scales, Wk_scales)
         load_codes(k_codes, Wk_words, 0)
         load_codes(q_codes, Wq_words, 2)
@@ -124,8 +125,7 @@ def tile_attention_pa_kernel(
                         identity[:],
                     )
             grouped = stage.tile([P, PASSES * P * 4], BF16, align_bytes=64)
-            copy = nc.vector.tensor_copy if t in (1, 3, 5) else nc.scalar.copy
-            copy(
+            nc.scalar.copy(
                 out=grouped[:].bitcast(F32).rearrange("p (c r u) -> p c r u", c=PASSES, u=2),
                 in_=planes[:].rearrange("p (c u) r -> p c r u", u=2),
             )
@@ -148,9 +148,9 @@ def tile_attention_pa_kernel(
                     stop=(c == PASSES - 1),
                 )
 
-        def multiply(products, slot, t, codes, plane, block, on_gpsimd=False):
+        def multiply(products, slot, t, block, on_gpsimd=False):
             bank = sums.tile([P, BANK], F32)
-            project(bank, t, codes, plane, block)
+            project(bank, t, q_codes, q_scales, block)
             engine = nc.vector
             if on_gpsimd:
                 copied = stage.tile([P, BANK], F32)
@@ -167,19 +167,29 @@ def tile_attention_pa_kernel(
                 op=MULT,
             )
 
-        def add(products, engine):
-            rotated = leaving.tile([P, PAIR * BANK_HEADS * 2, HALF], F32)
-            halves = products[:].rearrange("p s h e (u j) -> p (s h e) u j", u=2)
-            engine.tensor_tensor(out=rotated[:], in0=halves[:, :, 0, :], in1=halves[:, :, 1, :], op=ADD)
-            return rotated
+        def add_and_store(products, first, count, group, block):
+            rotated = leaving.tile([P, GROUP * BANK_HEADS * 2, HALF], F32)
+            rows = count * BANK_HEADS * 2
+            halves = products[:, first : first + count].rearrange("p s h e (u j) -> p (s h e) u j", u=2)
+            nc.gpsimd.tensor_tensor(
+                out=rotated[:, 0:rows, :], in0=halves[:, :, 0, :], in1=halves[:, :, 1, :], op=ADD
+            )
+            t = group * GROUP + first
+            nc.sync.dma_start(
+                out=q_rows[:, t : t + count, block * BANK : (block + 1) * BANK],
+                in_=rotated[:, 0:rows, :].rearrange("p (s g) j -> p s (g j)", s=count),
+            )
 
-        def add_bank(products, slot):
+        def add_bank_and_store(products, slot, group, block):
             rotated_bank = stage.tile([P, BANK_HEADS * 2, HALF], F32)
             halves = products[:, slot].rearrange("p h e (u j) -> p (h e) u j", u=2)
             nc.vector.tensor_tensor(
                 out=rotated_bank[:], in0=halves[:, :, 0, :], in1=halves[:, :, 1, :], op=ADD
             )
-            return rotated_bank
+            nc.sync.dma_start(
+                out=q_rows[:, group * GROUP + slot, block * BANK : (block + 1) * BANK],
+                in_=rotated_bank[:].rearrange("p g j -> p (g j)"),
+            )
 
         def turn_table(which, rows):
             planes = turned.tile([P, TILES, P], BF16)
@@ -228,69 +238,74 @@ def tile_attention_pa_kernel(
             )
 
         def new_products():
-            products = wide.tile([P, PAIR, BANK_HEADS, 2, HEAD], F32)
+            products = wide.tile([P, GROUP, BANK_HEADS, 2, HEAD], F32)
             return products
 
-        for t in range(4):
-            quantise_x(t)
+        def make_factors():
+            nc.vector.tensor_copy(out=factor[:, 0, 0], in_=cos_sb[:, :, 0:HALF])
+            nc.vector.tensor_scalar_mul(out=factor[:, 0, 1], in0=sin_sb[:, :, 0:HALF], scalar1=-1.0)
+            nc.vector.tensor_copy(out=factor[:, 1, 0], in_=sin_sb[:, :, HALF:HEAD])
+            nc.vector.tensor_copy(out=factor[:, 1, 1], in_=cos_sb[:, :, HALF:HEAD])
 
-        nc.vector.tensor_copy(out=factor[:, 0, 0], in_=cos_sb[:, :, 0:HALF])
-        nc.vector.tensor_scalar_mul(out=factor[:, 0, 1], in0=sin_sb[:, :, 0:HALF], scalar1=-1.0)
-        nc.vector.tensor_copy(out=factor[:, 1, 0], in_=sin_sb[:, :, HALF:HEAD])
-        nc.vector.tensor_copy(out=factor[:, 1, 1], in_=cos_sb[:, :, HALF:HEAD])
-
-        for t in range(4, 6):
-            quantise_x(t)
-        started = []
-        for t in range(EARLY):
-            started.append(new_products())
-            multiply(started[t], 0, t, q_codes, q_scales, 0)
-        for t in range(6, TILES):
-            quantise_x(t)
+        quantise_x(0)
+        quantise_x(1)
+        make_factors()
+        quantise_x(2)
+        quantise_x(3)
+        first_products = new_products()
+        multiply(first_products, 0, 0, 0)
+        multiply(first_products, 1, 1, 0)
+        quantise_x(4)
+        quantise_x(5)
+        multiply(first_products, 2, 2, 0)
+        multiply(first_products, 3, 3, 0)
+        quantise_x(6)
+        quantise_x(7)
 
         nc.scalar.copy(out=partner_sin[:, :, 0:HALF], in_=sin_sb[:, :, HALF:HEAD])
         nc.scalar.mul(out=partner_sin[:, :, HALF:HEAD], in_=sin_sb[:, :, 0:HALF], mul=-1.0)
 
+        units = [(block, group) for block in range(Q_BLOCKS) for group in range(TILES // GROUP)]
+        k_start = len(units)
+        last_step = 2 * len(units) - 1
         waiting = []
-        for sweep in range(Q_BLOCKS // PAIR):
-            for t in range(TILES):
-                if sweep == 1:
-                    both = multiply_upright(t // BANK_HEADS, t % BANK_HEADS)
-                if sweep == 0 and t < EARLY:
-                    products = started[t]
-                else:
-                    products = new_products()
-                    multiply(products, 0, t, q_codes, q_scales, sweep * PAIR)
-                for late in waiting:
-                    lay_down(late, (t - 1) // BANK_HEADS, (t - 1) % BANK_HEADS)
+        for unit, (block, group) in enumerate(units):
+            products = first_products if unit == 0 else new_products()
+            for half_unit in range(2):
+                step = 2 * unit + half_unit
+                slot = 2 * half_unit
+                if step >= k_start:
+                    k_group, k_head = divmod(step - k_start, BANK_HEADS)
+                    both = multiply_upright(k_group, k_head)
+                if unit > 0:
+                    multiply(products, slot, group * GROUP + slot, block, on_gpsimd=((unit, slot) in GPSIMD_MULTIPLIES))
+                for late, late_group, late_head in waiting:
+                    lay_down(late, late_group, late_head)
                 waiting = []
-                multiply(
-                    products, 1, t, q_codes, q_scales, sweep * PAIR + 1,
-                    on_gpsimd=(sweep == 1 and t in GPSIMD_MULTIPLIES),
-                )
-                if sweep == 1:
-                    waiting = [both]
-                if sweep == 1 and t == TILES - 1:
-                    lay_down(both, t // BANK_HEADS, t % BANK_HEADS)
-                columns = slice(sweep * PAIR * BANK, (sweep + 1) * PAIR * BANK)
-                if sweep == 1 and t == TILES - 1:
-                    for i in range(PAIR):
-                        rotated_bank = add_bank(products, i)
-                        nc.sync.dma_start(
-                            out=q_rows[:, t, columns.start + i * BANK : columns.start + (i + 1) * BANK],
-                            in_=rotated_bank[:].rearrange("p g j -> p (g j)"),
-                        )
-                else:
-                    rotated = add(products, nc.gpsimd)
-                    nc.sync.dma_start(out=q_rows[:, t, columns], in_=rotated[:].rearrange("p g j -> p (g j)"))
-                if sweep == 0 and t % PAIR == PAIR - 1:
+                if unit > 0:
+                    multiply(
+                        products, slot + 1, group * GROUP + slot + 1, block,
+                        on_gpsimd=((unit, slot + 1) in GPSIMD_MULTIPLIES),
+                    )
+                if step >= k_start:
+                    waiting = [(both, k_group, k_head)]
+                if step == last_step:
+                    lay_down(both, k_group, k_head)
+                if step == last_step:
+                    add_and_store(products, slot, 1, group, block)
+                    add_bank_and_store(products, slot + 1, group, block)
+                elif unit >= len(units) - FINE_UNITS:
+                    add_and_store(products, slot, 2, group, block)
+                elif half_unit == 1:
+                    add_and_store(products, 0, GROUP, group, block)
+                if step < TILES and step % PAIR == PAIR - 1:
                     v_out = stage.tile([P, PAIR, BANK], F32)
                     for i in range(PAIR):
                         v_bank = v_sums.tile([P, BANK], F32)
-                        project(v_bank, t + 1 - PAIR + i, v_codes, v_scales, 0)
+                        project(v_bank, step + 1 - PAIR + i, v_codes, v_scales, 0)
                         nc.scalar.copy(out=v_out[:, i, :], in_=v_bank[:])
-                    nc.scalar.dma_start(out=v_rows[:, t + 1 - PAIR : t + 1, :], in_=v_out[:])
-                if sweep == 0 and t == 2:
+                    nc.scalar.dma_start(out=v_rows[:, step + 1 - PAIR : step + 1, :], in_=v_out[:])
+                if step == 2:
                     turn_table(0, cos_sb)
-                if sweep == 0 and t == 4:
+                if step == 4:
                     turn_table(1, partner_sin)

@@ -258,9 +258,9 @@ def tile_attention_pa_kernel(
         quantise_x(4)
         quantise_x(5)
         multiply(first_products, 2, 2, 0)
-        multiply(first_products, 3, 3, 0)
         quantise_x(6)
         quantise_x(7)
+        multiply(first_products, 3, 3, 0)
 
         nc.scalar.copy(out=partner_sin[:, :, 0:HALF], in_=sin_sb[:, :, HALF:HEAD])
         nc.scalar.mul(out=partner_sin[:, :, HALF:HEAD], in_=sin_sb[:, :, 0:HALF], mul=-1.0)

@@ -25,7 +25,7 @@ BANK = 512
 BANK_HEADS = BANK // HEAD
 PAIR = 2
 GROUP = 4
-GPSIMD_MULTIPLIES = ((5, 3),)
+GPSIMD_MULTIPLIES = ((4, 0),)
 FINE_UNITS = 2
 Q_BLOCKS = 4
 QUADRANTS = 4
@@ -59,7 +59,7 @@ def tile_attention_pa_kernel(
         x_sb = keep.tile([P, TILES, HIDDEN], BF16)
         cos_sb = keep.tile([P, TILES, HEAD], BF16)
         sin_sb = keep.tile([P, TILES, HEAD], BF16)
-        factor = keep.tile([P, 2, 2, TILES, HALF], BF16)
+        factor = keep.tile([P, TILES // GROUP, 2, 2, GROUP, HALF], BF16)
         identity = keep.tile([P, P], F32)
         swap = keep.tile([P, P], F32)
         identity_bf = keep.tile([P, P], BF16)
@@ -70,7 +70,8 @@ def tile_attention_pa_kernel(
         q_codes = keep.tile([P, Q_BLOCKS, PASSES, BANK], U32, align_bytes=64)
         k_codes = keep.tile([P, 1, PASSES, BANK], U32, align_bytes=64)
         v_codes = keep.tile([P, 1, PASSES, BANK], U32, align_bytes=64)
-        q_scales = keep.tile([P, PASSES, Q_BLOCKS * BANK], U8, align_bytes=64)
+        q_scales_first = keep.tile([P, PASSES, BANK], U8, align_bytes=64)
+        q_scales_rest = keep.tile([P, PASSES, (Q_BLOCKS - 1) * BANK], U8, align_bytes=64)
         k_scales = keep.tile([P, PASSES, BANK], U8, align_bytes=64)
         v_scales = keep.tile([P, PASSES, BANK], U8, align_bytes=64)
 
@@ -83,30 +84,36 @@ def tile_attention_pa_kernel(
                 out=codes[:, block].bitcast(I32), in_=source[:, :, block * BANK : (block + 1) * BANK]
             )
 
-        def load_scales(plane, scales):
+        def load_scales(plane, scales, first, columns):
             nc.vector.memset(plane[:].bitcast(I32), 0)
             source = scales.bitcast(I32).rearrange("c s n -> s c n")
             for quadrant in range(QUADRANTS):
                 nc.sync.dma_start(
                     out=plane[32 * quadrant : 32 * quadrant + 4].bitcast(I32),
-                    in_=source[4 * quadrant : 4 * quadrant + 4],
+                    in_=source[4 * quadrant : 4 * quadrant + 4, :, first // 4 : (first + columns) // 4],
                 )
+
+        def load_tables(group):
+            tiles = slice(group * GROUP, (group + 1) * GROUP)
+            nc.sync.dma_start(out=cos_sb[:, tiles, :], in_=cos_rows[:, tiles, :])
+            nc.sync.dma_start(out=sin_sb[:, tiles, :], in_=sin_rows[:, tiles, :])
 
         make_identity(nc, identity[:])
         make_identity(nc, identity_bf[:])
         load_x(0, 1)
         load_x(1, 1)
         load_x(2, PAIR)
-        nc.sync.dma_start(out=cos_sb[:], in_=cos_rows)
-        nc.sync.dma_start(out=sin_sb[:], in_=sin_rows)
+        load_tables(0)
         load_codes(q_codes, Wq_words, 0)
-        load_scales(q_scales, Wq_scales)
+        load_scales(q_scales_first, Wq_scales, 0, BANK)
         load_x(4, PAIR)
         load_x(6, PAIR)
-        load_scales(v_scales, Wv_scales)
+        load_tables(1)
+        load_scales(v_scales, Wv_scales, 0, BANK)
         load_codes(v_codes, Wv_words, 0)
+        load_scales(q_scales_rest, Wq_scales, BANK, (Q_BLOCKS - 1) * BANK)
         load_codes(q_codes, Wq_words, 1)
-        load_scales(k_scales, Wk_scales)
+        load_scales(k_scales, Wk_scales, 0, BANK)
         load_codes(k_codes, Wk_words, 0)
         load_codes(q_codes, Wq_words, 2)
         load_codes(q_codes, Wq_words, 3)
@@ -136,21 +143,24 @@ def tile_attention_pa_kernel(
                     in_=grouped[:, c * K_PASS : (c + 1) * K_PASS],
                 )
 
-        def project(bank, t, codes, plane, block):
+        def project(bank, t, codes, block, plane, plane_block):
             for c in range(PASSES):
                 nc.tensor.matmul_mx(
                     out=bank[:],
                     lhsT=x_codes[:, c, t * P : (t + 1) * P].bitcast(FP8X4),
                     lhsT_scale=x_scales[:, c, t * P : (t + 1) * P],
                     rhs=codes[:, block, c, :].bitcast(FP8X4),
-                    rhs_scale=plane[:, c, block * BANK : (block + 1) * BANK],
+                    rhs_scale=plane[:, c, plane_block * BANK : (plane_block + 1) * BANK],
                     start=(c == 0),
                     stop=(c == PASSES - 1),
                 )
 
         def multiply(products, slot, t, block, on_gpsimd=False):
             bank = sums.tile([P, BANK], F32)
-            project(bank, t, q_codes, q_scales, block)
+            if block == 0:
+                project(bank, t, q_codes, block, q_scales_first, 0)
+            else:
+                project(bank, t, q_codes, block, q_scales_rest, block - 1)
             engine = nc.vector
             if on_gpsimd:
                 copied = stage.tile([P, BANK], F32)
@@ -163,7 +173,7 @@ def tile_attention_pa_kernel(
                 .rearrange("p (h u j) -> p h u j", u=2, j=HALF)
                 .unsqueeze(2)
                 .to_broadcast([P, BANK_HEADS, 2, 2, HALF]),
-                in1=factor[:, :, :, t, :].unsqueeze(1).to_broadcast([P, BANK_HEADS, 2, 2, HALF]),
+                in1=factor[:, t // GROUP, :, :, t % GROUP, :].unsqueeze(1).to_broadcast([P, BANK_HEADS, 2, 2, HALF]),
                 op=MULT,
             )
 
@@ -241,15 +251,16 @@ def tile_attention_pa_kernel(
             products = wide.tile([P, GROUP, BANK_HEADS, 2, HEAD], F32)
             return products
 
-        def make_factors():
-            nc.vector.tensor_copy(out=factor[:, 0, 0], in_=cos_sb[:, :, 0:HALF])
-            nc.vector.tensor_scalar_mul(out=factor[:, 0, 1], in0=sin_sb[:, :, 0:HALF], scalar1=-1.0)
-            nc.vector.tensor_copy(out=factor[:, 1, 0], in_=sin_sb[:, :, HALF:HEAD])
-            nc.vector.tensor_copy(out=factor[:, 1, 1], in_=cos_sb[:, :, HALF:HEAD])
+        def make_factors(group):
+            tiles = slice(group * GROUP, (group + 1) * GROUP)
+            nc.vector.tensor_copy(out=factor[:, group, 0, 0], in_=cos_sb[:, tiles, 0:HALF])
+            nc.vector.tensor_scalar_mul(out=factor[:, group, 0, 1], in0=sin_sb[:, tiles, 0:HALF], scalar1=-1.0)
+            nc.vector.tensor_copy(out=factor[:, group, 1, 0], in_=sin_sb[:, tiles, HALF:HEAD])
+            nc.vector.tensor_copy(out=factor[:, group, 1, 1], in_=cos_sb[:, tiles, HALF:HEAD])
 
         quantise_x(0)
         quantise_x(1)
-        make_factors()
+        make_factors(0)
         quantise_x(2)
         quantise_x(3)
         first_products = new_products()
@@ -261,6 +272,7 @@ def tile_attention_pa_kernel(
         quantise_x(6)
         quantise_x(7)
         multiply(first_products, 3, 3, 0)
+        make_factors(1)
 
         nc.scalar.copy(out=partner_sin[:, :, 0:HALF], in_=sin_sb[:, :, HALF:HEAD])
         nc.scalar.mul(out=partner_sin[:, :, HALF:HEAD], in_=sin_sb[:, :, 0:HALF], mul=-1.0)
@@ -302,7 +314,7 @@ def tile_attention_pa_kernel(
                     v_out = stage.tile([P, PAIR, BANK], F32)
                     for i in range(PAIR):
                         v_bank = v_sums.tile([P, BANK], F32)
-                        project(v_bank, step + 1 - PAIR + i, v_codes, v_scales, 0)
+                        project(v_bank, step + 1 - PAIR + i, v_codes, 0, v_scales, 0)
                         nc.scalar.copy(out=v_out[:, i, :], in_=v_bank[:])
                     nc.scalar.dma_start(out=v_rows[:, step + 1 - PAIR : step + 1, :], in_=v_out[:])
                 if step == 2:

@@ -102,10 +102,10 @@ def tile_attention_pa_kernel(
         make_identity(nc, identity_bf[:])
         load_x(0, 1)
         load_x(1, 1)
+        load_scales(q_scales_first, Wq_scales, 0, BANK)
         load_x(2, PAIR)
         load_tables(0)
         load_codes(q_codes, Wq_words, 0)
-        load_scales(q_scales_first, Wq_scales, 0, BANK)
         load_x(4, PAIR)
         load_x(6, PAIR)
         load_tables(1)

@@ -25,6 +25,7 @@ BANK = 512
 BANK_HEADS = BANK // HEAD
 PAIR = 2
 GROUP = 4
+V_STEPS = (2, 4, 6, 7)
 GPSIMD_MULTIPLIES = ((4, 0),)
 FINE_UNITS = 2
 Q_BLOCKS = 4
@@ -310,14 +311,15 @@ def tile_attention_pa_kernel(
                     add_and_store(products, slot, 2, group, block)
                 elif half_unit == 1:
                     add_and_store(products, 0, GROUP, group, block)
-                if step < TILES and step % PAIR == PAIR - 1:
+                if step in V_STEPS:
+                    v_first = PAIR * V_STEPS.index(step)
                     v_out = stage.tile([P, PAIR, BANK], F32)
                     for i in range(PAIR):
                         v_bank = v_sums.tile([P, BANK], F32)
-                        project(v_bank, step + 1 - PAIR + i, v_codes, 0, v_scales, 0)
+                        project(v_bank, v_first + i, v_codes, 0, v_scales, 0)
                         nc.scalar.copy(out=v_out[:, i, :], in_=v_bank[:])
-                    nc.scalar.dma_start(out=v_rows[:, step + 1 - PAIR : step + 1, :], in_=v_out[:])
-                if step == 2:
+                    nc.scalar.dma_start(out=v_rows[:, v_first : v_first + PAIR, :], in_=v_out[:])
+                if step == 3:
                     turn_table(0, cos_sb)
-                if step == 4:
+                if step == 5:
                     turn_table(1, partner_sin)

@@ -272,8 +272,8 @@ def tile_attention_pa_kernel(
         multiply(first_products, 2, 2, 0)
         quantise_x(6)
         quantise_x(7)
-        multiply(first_products, 3, 3, 0)
         make_factors(1)
+        multiply(first_products, 3, 3, 0)
 
         nc.scalar.copy(out=partner_sin[:, :, 0:HALF], in_=sin_sb[:, :, HALF:HEAD])
         nc.scalar.mul(out=partner_sin[:, :, HALF:HEAD], in_=sin_sb[:, :, 0:HALF], mul=-1.0)

@@ -53,8 +53,7 @@ def tile_attention_pa_kernel(
         upright = ctx.enter_context(tc.tile_pool(name="upright", bufs=3))
         leaving = ctx.enter_context(tc.tile_pool(name="leaving", bufs=3))
         turned = ctx.enter_context(tc.psum_pool(name="turned", bufs=2))
-        sums = ctx.enter_context(tc.psum_pool(name="sums", bufs=4))
-        v_sums = ctx.enter_context(tc.psum_pool(name="v_sums", bufs=2))
+        sums = ctx.enter_context(tc.psum_pool(name="sums", bufs=6))
         ctx.enter_context(tc.manual_schedule())
 
         x_sb = keep.tile([P, TILES, HIDDEN], BF16)
@@ -315,9 +314,9 @@ def tile_attention_pa_kernel(
                     v_first = PAIR * V_STEPS.index(step)
                     v_out = stage.tile([P, PAIR, BANK], F32)
                     for i in range(PAIR):
-                        v_bank = v_sums.tile([P, BANK], F32)
-                        project(v_bank, v_first + i, v_codes, 0, v_scales, 0)
-                        nc.scalar.copy(out=v_out[:, i, :], in_=v_bank[:])
+                        bank = sums.tile([P, BANK], F32)
+                        project(bank, v_first + i, v_codes, 0, v_scales, 0)
+                        nc.scalar.copy(out=v_out[:, i, :], in_=bank[:])
                     nc.scalar.dma_start(out=v_rows[:, v_first : v_first + PAIR, :], in_=v_out[:])
                 if step == 3:
                     turn_table(0, cos_sb)

from contextlib import ExitStack

import concourse.mybir as mybir
from concourse.masks import make_identity

F32 = mybir.dt.float32
BF16 = mybir.dt.bfloat16
I32 = mybir.dt.int32
U32 = mybir.dt.uint32
U8 = mybir.dt.uint8
FP8X4 = mybir.dt.float8_e4m3fn_x4
MULT = mybir.AluOpType.mult
ADD = mybir.AluOpType.add

P = 128
TOKENS = 1024
HIDDEN = 1024
TILES = TOKENS // P
K_PASS = 4 * P
PASSES = HIDDEN // K_PASS
WORDS = K_PASS // 2
HEAD = 128
HALF = HEAD // 2
BANK = 512
BANK_HEADS = BANK // HEAD
PAIR = 2
GROUP = 4
V_STEPS = (2, 4, 6, 7)
GPSIMD_MULTIPLIES = ((4, 0),)
FINE_UNITS = 2
Q_BLOCKS = 4
QUADRANTS = 4

FLOPS = 2 * TOKENS * HIDDEN * (Q_BLOCKS + 2) * BANK


def tile_attention_pa_kernel(
    tc, x, cos, sin, Wq_words, Wq_scales, Wk_words, Wk_scales, Wv_words, Wv_scales, out_0, out_1, out_2
):
    nc = tc.nc

    x_rows = x.rearrange("o (r t) k -> r (o t) k", t=TILES)
    cos_rows = cos.rearrange("(r t) d -> r t d", t=TILES)
    sin_rows = sin.rearrange("(r t) d -> r t d", t=TILES)
    q_rows = out_0.rearrange("o (r t) h d -> r (o t) (h d)", t=TILES)
    k_rows = out_1.rearrange("o (r t) h d -> r (o t) (h d)", t=TILES)
    v_rows = out_2.rearrange("o (r t) h d -> r (o t) (h d)", t=TILES)

    with ExitStack() as ctx:
        keep = ctx.enter_context(tc.tile_pool(name="keep", bufs=1))
        stage = ctx.enter_context(tc.tile_pool(name="stage", bufs=3))
        wide = ctx.enter_context(tc.tile_pool(name="wide", bufs=5))
        upright = ctx.enter_context(tc.tile_pool(name="upright", bufs=3))
        leaving = ctx.enter_context(tc.tile_pool(name="leaving", bufs=3))
        turned = ctx.enter_context(tc.psum_pool(name="turned", bufs=2))
        sums = ctx.enter_context(tc.psum_pool(name="sums", bufs=6))
        ctx.enter_context(tc.manual_schedule())

        x_sb = keep.tile([P, TILES, HIDDEN], BF16)
        cos_sb = keep.tile([P, TILES, HEAD], BF16)
        sin_sb = keep.tile([P, TILES, HEAD], BF16)
        factor = keep.tile([P, TILES // GROUP, 2, 2, GROUP, HALF], BF16)
        identity = keep.tile([P, P], F32)
        swap = keep.tile([P, P], F32)
        identity_bf = keep.tile([P, P], BF16)
        partner_sin = keep.tile([P, TILES, HEAD], BF16)
        tables = keep.tile([P, 2, TOKENS], BF16)
        x_codes = keep.tile([P, PASSES, TOKENS], U32, align_bytes=64)
        x_scales = keep.tile([P, PASSES, TOKENS], U8, align_bytes=64)
        q_codes = keep.tile([P, Q_BLOCKS, PASSES, BANK], U32, align_bytes=64)
        k_codes = keep.tile([P, 1, PASSES, BANK], U32, align_bytes=64)
        v_codes = keep.tile([P, 1, PASSES, BANK], U32, align_bytes=64)
        q_scales_first = keep.tile([P, PASSES, BANK], U8, align_bytes=64)
        q_scales_rest = keep.tile([P, PASSES, (Q_BLOCKS - 1) * BANK], U8, align_bytes=64)
        k_scales = keep.tile([P, PASSES, BANK], U8, align_bytes=64)
        v_scales = keep.tile([P, PASSES, BANK], U8, align_bytes=64)

        def load_x(t, count):
            nc.sync.dma_start(out=x_sb[:, t : t + count, :], in_=x_rows[:, t : t + count, :])

        def load_codes(codes, words, block):
            source = words.bitcast(I32).rearrange("c p n o -> p c (n o)")
            nc.sync.dma_start(
                out=codes[:, block].bitcast(I32), in_=source[:, :, block * BANK : (block + 1) * BANK]
            )

        def load_scales(plane, scales, first, columns):
            nc.vector.memset(plane[:].bitcast(I32), 0)
            source = scales.bitcast(I32).rearrange("c s n -> s c n")
            for quadrant in range(QUADRANTS):
                nc.sync.dma_start(
                    out=plane[32 * quadrant : 32 * quadrant + 4].bitcast(I32),
                    in_=source[4 * quadrant : 4 * quadrant + 4, :, first // 4 : (first + columns) // 4],
                )

        def load_tables(group):
            tiles = slice(group * GROUP, (group + 1) * GROUP)
            nc.sync.dma_start(out=cos_sb[:, tiles, :], in_=cos_rows[:, tiles, :])
            nc.sync.dma_start(out=sin_sb[:, tiles, :], in_=sin_rows[:, tiles, :])

        make_identity(nc, identity[:])
        make_identity(nc, identity_bf[:])
        load_x(0, 1)
        load_x(1, 1)
        load_scales(q_scales_first, Wq_scales, 0, BANK)
        load_x(2, PAIR)
        load_tables(0)
        load_codes(q_codes, Wq_words, 0)
        load_x(4, PAIR)
        load_x(6, PAIR)
        load_tables(1)
        load_scales(v_scales, Wv_scales, 0, BANK)
        load_codes(v_codes, Wv_words, 0)
        load_scales(q_scales_rest, Wq_scales, BANK, (Q_BLOCKS - 1) * BANK)
        load_codes(q_codes, Wq_words, 1)
        load_scales(k_scales, Wk_scales, 0, BANK)
        load_codes(k_codes, Wk_words, 0)
        load_codes(q_codes, Wq_words, 2)
        load_codes(q_codes, Wq_words, 3)
        nc.vector.tensor_copy(out=swap[:, 0:HALF], in_=identity[:, HALF:P])
        nc.vector.tensor_copy(out=swap[:, HALF:P], in_=identity[:, 0:HALF])

        x_words = x_sb[:].bitcast(F32)

        def quantise_x(t):
            planes = turned.tile([P, PASSES * 2, P], F32)
            for c in range(PASSES):
                for u in range(2):
                    nc.tensor.transpose(
                        planes[:, 2 * c + u, :],
                        x_words[:, t, WORDS * c + u : WORDS * (c + 1) : 2],
                        identity[:],
                    )
            grouped = stage.tile([P, PASSES * P * 4], BF16, align_bytes=64)
            nc.scalar.copy(
                out=grouped[:].bitcast(F32).rearrange("p (c r u) -> p c r u", c=PASSES, u=2),
                in_=planes[:].rearrange("p (c u) r -> p c r u", u=2),
            )
            for c in range(PASSES):
                nc.vector.quantize_mx(
                    out=x_codes[:, c, t * P : (t + 1) * P].bitcast(FP8X4),
                    scales=x_scales[:, c, t * P : (t + 1) * P],
                    in_=grouped[:, c * K_PASS : (c + 1) * K_PASS],
                )

        def project(bank, t, codes, block, plane, plane_block):
            for c in range(PASSES):
                nc.tensor.matmul_mx(
                    out=bank[:],
                    lhsT=x_codes[:, c, t * P : (t + 1) * P].bitcast(FP8X4),
                    lhsT_scale=x_scales[:, c, t * P : (t + 1) * P],
                    rhs=codes[:, block, c, :].bitcast(FP8X4),
                    rhs_scale=plane[:, c, plane_block * BANK : (plane_block + 1) * BANK],
                    start=(c == 0),
                    stop=(c == PASSES - 1),
                )

        def multiply(products, slot, t, block, on_gpsimd=False):
            bank = sums.tile([P, BANK], F32)
            if block == 0:
                project(bank, t, q_codes, block, q_scales_first, 0)
            else:
                project(bank, t, q_codes, block, q_scales_rest, block - 1)
            engine = nc.vector
            if on_gpsimd:
                copied = stage.tile([P, BANK], F32)
                nc.scalar.copy(out=copied[:], in_=bank[:])
                bank = copied
                engine = nc.gpsimd
            engine.tensor_tensor(
                out=products[:, slot].rearrange("p h e (u j) -> p h e u j", u=2),
                in0=bank[:]
                .rearrange("p (h u j) -> p h u j", u=2, j=HALF)
                .unsqueeze(2)
                .to_broadcast([P, BANK_HEADS, 2, 2, HALF]),
                in1=factor[:, t // GROUP, :, :, t % GROUP, :].unsqueeze(1).to_broadcast([P, BANK_HEADS, 2, 2, HALF]),
                op=MULT,
            )

        def add_and_store(products, first, count, group, block):
            rotated = leaving.tile([P, GROUP * BANK_HEADS * 2, HALF], F32)
            rows = count * BANK_HEADS * 2
            halves = products[:, first : first + count].rearrange("p s h e (u j) -> p (s h e) u j", u=2)
            nc.gpsimd.tensor_tensor(
                out=rotated[:, 0:rows, :], in0=halves[:, :, 0, :], in1=halves[:, :, 1, :], op=ADD
            )
            t = group * GROUP + first
            nc.sync.dma_start(
                out=q_rows[:, t : t + count, block * BANK : (block + 1) * BANK],
                in_=rotated[:, 0:rows, :].rearrange("p (s g) j -> p s (g j)", s=count),
            )

        def add_bank_and_store(products, slot, group, block):
            rotated_bank = stage.tile([P, BANK_HEADS * 2, HALF], F32)
            halves = products[:, slot].rearrange("p h e (u j) -> p (h e) u j", u=2)
            nc.vector.tensor_tensor(
                out=rotated_bank[:], in0=halves[:, :, 0, :], in1=halves[:, :, 1, :], op=ADD
            )
            nc.sync.dma_start(
                out=q_rows[:, group * GROUP + slot, block * BANK : (block + 1) * BANK],
                in_=rotated_bank[:].rearrange("p g j -> p (g j)"),
            )

        def turn_table(which, rows):
            planes = turned.tile([P, TILES, P], BF16)
            for t in range(TILES):
                nc.tensor.transpose(planes[:, t, :], rows[:, t, :], identity_bf[:])
            nc.scalar.copy(out=tables[:, which, :], in_=planes[:].rearrange("p t r -> p (t r)"))

        def multiply_upright(group, head):
            bank = sums.tile([P, BANK], F32)
            tokens = slice(group * BANK, (group + 1) * BANK)
            for c in range(PASSES):
                nc.tensor.matmul_mx(
                    out=bank[:],
                    lhsT=k_codes[:, 0, c, head * P : (head + 1) * P].bitcast(FP8X4),
                    lhsT_scale=k_scales[:, c, head * P : (head + 1) * P],
                    rhs=x_codes[:, c, tokens].bitcast(FP8X4),
                    rhs_scale=x_scales[:, c, tokens],
                    start=(c == 0),
                    stop=(c == PASSES - 1),
                )
            both = upright.tile([P, 2, BANK], F32)
            nc.vector.tensor_tensor(
                out=both[:],
                in0=bank[:].unsqueeze(1).to_broadcast([P, 2, BANK]),
                in1=tables[:, :, tokens],
                op=MULT,
            )
            return both

        def lay_down(both, group, head):
            planes = turned.tile([P, BANK_HEADS, P], F32)
            for i in range(BANK_HEADS):
                nc.tensor.matmul(
                    out=planes[:, i, :], lhsT=both[:, 0, i * P : (i + 1) * P], rhs=identity[:],
                    is_transpose=True, start=True, stop=False,
                )
                nc.tensor.matmul(
                    out=planes[:, i, :], lhsT=both[:, 1, i * P : (i + 1) * P], rhs=swap[:],
                    is_transpose=True, start=False, stop=True,
                )
            k_part = stage.tile([P, BANK_HEADS, P], F32)
            nc.scalar.copy(out=k_part[:], in_=planes[:])
            nc.scalar.dma_start(
                out=k_rows[:, group * BANK_HEADS : (group + 1) * BANK_HEADS, head * P : (head + 1) * P],
                in_=k_part[:],
            )

        def new_products():
            products = wide.tile([P, GROUP, BANK_HEADS, 2, HEAD], F32)
            return products

        def make_factors(group):
            tiles = slice(group * GROUP, (group + 1) * GROUP)
            nc.vector.tensor_copy(out=factor[:, group, 0, 0], in_=cos_sb[:, tiles, 0:HALF])
            nc.vector.tensor_scalar_mul(out=factor[:, group, 0, 1], in0=sin_sb[:, tiles, 0:HALF], scalar1=-1.0)
            nc.vector.tensor_copy(out=factor[:, group, 1, 0], in_=sin_sb[:, tiles, HALF:HEAD])
            nc.vector.tensor_copy(out=factor[:, group, 1, 1], in_=cos_sb[:, tiles, HALF:HEAD])

        quantise_x(0)
        quantise_x(1)
        make_factors(0)
        quantise_x(2)
        quantise_x(3)
        first_products = new_products()
        multiply(first_products, 0, 0, 0)
        multiply(first_products, 1, 1, 0)
        quantise_x(4)
        quantise_x(5)
        multiply(first_products, 2, 2, 0)
        quantise_x(6)
        quantise_x(7)
        make_factors(1)
        multiply(first_products, 3, 3, 0)

        nc.scalar.copy(out=partner_sin[:, :, 0:HALF], in_=sin_sb[:, :, HALF:HEAD])
        nc.scalar.mul(out=partner_sin[:, :, HALF:HEAD], in_=sin_sb[:, :, 0:HALF], mul=-1.0)

        units = [(block, group) for block in range(Q_BLOCKS) for group in range(TILES // GROUP)]
        k_start = len(units)
        last_step = 2 * len(units) - 1
        waiting = []
        for unit, (block, group) in enumerate(units):
            products = first_products if unit == 0 else new_products()
            for half_unit in range(2):
                step = 2 * unit + half_unit
                slot = 2 * half_unit
                if step >= k_start:
                    k_group, k_head = divmod(step - k_start, BANK_HEADS)
                    both = multiply_upright(k_group, k_head)
                if unit > 0:
                    multiply(products, slot, group * GROUP + slot, block, on_gpsimd=((unit, slot) in GPSIMD_MULTIPLIES))
                for late, late_group, late_head in waiting:
                    lay_down(late, late_group, late_head)
                waiting = []
                if unit > 0:
                    multiply(
                        products, slot + 1, group * GROUP + slot + 1, block,
                        on_gpsimd=((unit, slot + 1) in GPSIMD_MULTIPLIES),
                    )
                if step >= k_start:
                    waiting = [(both, k_group, k_head)]
                if step == last_step:
                    lay_down(both, k_group, k_head)
                if step == last_step:
                    add_and_store(products, slot, 1, group, block)
                    add_bank_and_store(products, slot + 1, group, block)
                elif unit >= len(units) - FINE_UNITS:
                    add_and_store(products, slot, 2, group, block)
                elif half_unit == 1:
                    add_and_store(products, 0, GROUP, group, block)
                if step in V_STEPS:
                    v_first = PAIR * V_STEPS.index(step)
                    v_out = stage.tile([P, PAIR, BANK], F32)
                    for i in range(PAIR):
                        bank = sums.tile([P, BANK], F32)
                        project(bank, v_first + i, v_codes, 0, v_scales, 0)
                        nc.scalar.copy(out=v_out[:, i, :], in_=bank[:])
                    nc.scalar.dma_start(out=v_rows[:, v_first : v_first + PAIR, :], in_=v_out[:])
                if step == 3:
                    turn_table(0, cos_sb)
                if step == 5:
                    turn_table(1, partner_sin)
